import numpy as np
import ml_dtypes


def mxq(x, axis, fmt="e4m3"):
    dtype, down = {"e4m3": (ml_dtypes.float8_e4m3fn, 7), "e5m2": (ml_dtypes.float8_e5m2, 14)}[fmt]
    v = np.moveaxis(np.asarray(x, np.float32).astype(ml_dtypes.bfloat16).astype(np.float64), axis, -1)
    blocks = v.reshape(v.shape[:-1] + (-1, 32))
    amax = np.abs(blocks).max(-1, keepdims=True)
    byte = np.maximum(np.where(amax > 0, np.frexp(amax)[1] - 1 + 127, 0) - down, 1)
    scale = np.exp2(byte - 127.0)
    codes = (blocks / scale).astype(np.float32).astype(dtype).astype(np.float64)
    return np.moveaxis((codes * scale).reshape(v.shape), -1, axis)


WIDE = False


def mx_kscale(k):
    if not WIDE:
        return np.ones(k)
    levels = np.array([20, -20, 10, -10, 0])
    a = np.random.permutation(np.resize(levels, k // 512 * 4)).reshape(k // 512, 4)
    idx = np.arange(k)
    return np.exp2(a[idx // 512, idx % 128 // 32])


BF16 = ml_dtypes.bfloat16


def bf(x):
    return np.asarray(x, np.float32).astype(BF16)


def f64(x):
    return np.asarray(x).astype(np.float64)


M, K, N, R = 2048, 512, 512, 16


def mix(rows, u, a, b):
    return a * (np.random.standard_normal((rows, R)) @ u) / np.sqrt(R) + b * np.random.standard_normal((rows, K))


def setup_inputs():
    v = mx_kscale(N)
    u = np.random.standard_normal((R, K))
    x = bf(mix(M, u, 1.0, 0.5))
    w0 = bf(mix(N, u, 1.0, 0.5) * (np.sqrt(R) / K))
    bias = bf(np.random.standard_normal(N) * 0.3)
    center = bf(mix(N, u, 0.5, 0.1))
    sigma0 = bf(np.sqrt(K) * (1.0 + 0.1 * np.random.standard_normal(N)))
    g = bf(np.random.standard_normal((M, N)) * np.exp2(np.random.randint(-12, 1, (M, 1))) * 64.0 * v)
    xf, wf, bfl, cf, sf = f64(x), f64(w0), f64(bias), f64(center), f64(sigma0)
    pw = xf @ wf.T + bfl
    wn = wf / np.maximum(np.sqrt(np.sum(wf * wf, axis=1, keepdims=True)), 1e-12)
    pwc = xf @ wn.T - np.sum(cf * wn, axis=1)
    xn = np.sum(xf * xf, axis=1, keepdims=True) + np.sum(cf * cf, axis=1) - 2.0 * (xf @ cf.T)
    om = np.exp(-(xn - pwc * pwc) / (sf * sf))
    return {"x": x,
            "weights": bf(f64(w0) / v[:, None]),
            "bias": bias,
            "center": center,
            "sigma": bf(f64(sigma0) * np.sqrt(v)),
            "pw": np.asarray(pw, np.float32),
            "pwc": np.asarray(pwc, np.float32),
            "om": np.asarray(om, np.float32),
            "grad_out": g}


def reference(x, weights, bias, center, sigma, pw, pwc, om, grad_out):
    x, weights, center, sigma = f64(x), f64(weights), f64(center), f64(sigma)
    pw, pwc, om, g = f64(pw), f64(pwc), f64(om), f64(grad_out)
    wnorm = np.maximum(np.sqrt(np.sum(weights * weights, axis=1)), 1e-12)
    ga = g * om
    h = ga * pw / (sigma * sigma)
    d = ga + 2.0 * pwc * h / wnorm
    t1 = mxq(d, 1, "e5m2") @ mxq(weights, 0, "e4m3")
    t2 = mxq(h, 1, "e5m2") @ mxq(center, 0, "e4m3")
    return t1 + 2.0 * t2 - 2.0 * x * np.sum(h, axis=1, keepdims=True)

@@ -1,0 +1,209 @@
+from contextlib import ExitStack
+
+import concourse.mybir as mybir
+from concourse.masks import make_identity
+
+F32 = mybir.dt.float32
+BF16 = mybir.dt.bfloat16
+U32 = mybir.dt.uint32
+U8 = mybir.dt.uint8
+E4M3_X4 = mybir.dt.float8_e4m3fn_x4
+E5M2_X4 = mybir.dt.float8_e5m2_x4
+MULT = mybir.AluOpType.mult
+ADD = mybir.AluOpType.add
+ACT = mybir.ActivationFunctionType
+
+P = 128
+TOKENS = 2048
+F_OUT = 512
+F_IN = 512
+PACK = 4
+TILES = TOKENS // P
+CHUNK = 2
+CHUNKS = TILES // CHUNK
+SUM_COLS = 64
+
+FLOPS = 2 * 2 * TOKENS * F_OUT * F_IN
+
+
+def tile_orthogonallyattenuatedlinear_t_v_kernel(
+    tc, x, weights, bias, center, sigma, pw, pwc, om, grad_out, out
+):
+    nc = tc.nc
+
+    def by_token_tile(ap):
+        return ap.rearrange("(q j) f -> q j f", j=TILES)
+
+    with ExitStack() as stack:
+        consts = stack.enter_context(tc.tile_pool(name="consts", bufs=1))
+        inputs = stack.enter_context(tc.tile_pool(name="inputs", bufs=1))
+        work = stack.enter_context(tc.tile_pool(name="work", bufs=3))
+        results = stack.enter_context(tc.tile_pool(name="results", bufs=3))
+        flipped = stack.enter_context(tc.psum_pool(name="flipped", bufs=2))
+        sums = stack.enter_context(tc.psum_pool(name="sums", bufs=1))
+
+        sigma_rows_bf = consts.tile([P, P], BF16)
+        nc.vector.memset(sigma_rows_bf[:], 0.0)
+        nc.sync.dma_start(out=sigma_rows_bf[0:PACK, :], in_=sigma.rearrange("(b q) -> b q", q=P))
+
+        w_raw = consts.tile([P, PACK, F_IN], BF16)
+        c_raw = consts.tile([P, PACK, F_IN], BF16)
+        g_in, om_in, pw_in, pwc_in, x_in = [], [], [], [], []
+        for c in range(CHUNKS):
+            tiles_of_chunk = slice(c * CHUNK, (c + 1) * CHUNK)
+            for held, source, dtype, label in (
+                (g_in, grad_out, BF16, "g"),
+                (om_in, om, F32, "om"),
+                (pw_in, pw, F32, "pw"),
+                (pwc_in, pwc, F32, "pwc"),
+                (x_in, x, BF16, "x"),
+            ):
+                loaded = inputs.tile([P, CHUNK, F_OUT], dtype, name="%s%d" % (label, c))
+                nc.sync.dma_start(out=loaded[:], in_=by_token_tile(source)[:, tiles_of_chunk, :])
+                held.append(loaded)
+                if c == 0 and label == "om":
+                    nc.sync.dma_start(out=w_raw[:], in_=weights.rearrange("(b q) k -> q b k", q=P))
+                if c == 0 and label == "pwc":
+                    nc.sync.dma_start(out=c_raw[:], in_=center.rearrange("(b q) k -> q b k", q=P))
+
+        identity = consts.tile([P, P], F32)
+        make_identity(nc, identity[:])
+        minus_ones = consts.tile([P, SUM_COLS], F32)
+        nc.vector.memset(minus_ones[:], -1.0)
+
+        warm = consts.tile([P, 1], F32)
+        nc.vector.memset(warm[:], 1.0)
+        nc.scalar.sqrt(out=warm[:], in_=warm[:])
+
+        sigma_rows = consts.tile([P, P], F32)
+        nc.vector.tensor_copy(out=sigma_rows[:], in_=sigma_rows_bf[:])
+        sigma_flipped = flipped.tile([P, PACK, P], F32, tag="t_flipped")
+        nc.tensor.transpose(sigma_flipped[:, 0, :], sigma_rows[:], identity[:])
+        sigma_cols = consts.tile([P, PACK], F32)
+        nc.vector.tensor_copy(out=sigma_cols[:], in_=sigma_flipped[:, 0, 0:PACK])
+        half_sigma2 = consts.tile([P, PACK], F32)
+        nc.vector.scalar_tensor_tensor(
+            out=half_sigma2[:], in0=sigma_cols[:], scalar=0.5, in1=sigma_cols[:], op0=MULT, op1=MULT
+        )
+        two_over_sigma2 = consts.tile([P, PACK], F32)
+        nc.vector.reciprocal(out=two_over_sigma2[:], in_=half_sigma2[:])
+
+        squares = consts.tile([P, PACK, F_IN], BF16)
+        sum_squares = consts.tile([P, PACK], F32)
+        for b in range(PACK):
+            nc.scalar.activation(
+                out=squares[:, b, :], in_=w_raw[:, b, :], func=ACT.Square,
+                accum_out=sum_squares[:, b : b + 1],
+            )
+        wnorm = consts.tile([P, PACK], F32)
+        nc.scalar.sqrt(out=wnorm[:], in_=sum_squares[:])
+        wnorm_floor = consts.tile([P, PACK], F32)
+        nc.vector.tensor_scalar_max(out=wnorm_floor[:], in0=wnorm[:], scalar1=1e-12)
+        one_over_wnorm = consts.tile([P, PACK], F32)
+        nc.vector.reciprocal(out=one_over_wnorm[:], in_=wnorm_floor[:])
+
+        def quantise_matrix(raw, label):
+            grouped = consts.tile([P, F_IN, PACK], BF16, align_bytes=64, name=label + "_grouped")
+            nc.vector.tensor_copy(out=grouped[:], in_=raw[:].rearrange("q b k -> q k b"))
+            codes = consts.tile([P, F_IN], U32, align_bytes=64, name=label + "_codes")
+            scales = consts.tile([P, F_IN], U8, align_bytes=64, name=label + "_scales")
+            nc.vector.quantize_mx(
+                out=codes[:].bitcast(E4M3_X4), scales=scales[:],
+                in_=grouped[:].rearrange("q k b -> q (k b)"),
+            )
+            return codes, scales
+
+        w_codes, w_scales = quantise_matrix(w_raw, "w")
+        c_codes, c_scales = quantise_matrix(c_raw, "c")
+
+        live = {}
+
+        def products_and_transposes(j):
+            c, i = divmod(j, CHUNK)
+            ga = work.tile([P, F_OUT], F32, tag="ga")
+            nc.gpsimd.tensor_tensor(out=ga[:], in0=g_in[c][:, i, :], in1=om_in[c][:, i, :], op=MULT)
+            gapw = work.tile([P, F_OUT], F32, tag="gapw")
+            nc.gpsimd.tensor_tensor(out=gapw[:], in0=ga[:], in1=pw_in[c][:, i, :], op=MULT)
+            pwc_flipped = flipped.tile([P, PACK, P], F32, tag="pwc_flipped")
+            ga_flipped = flipped.tile([P, PACK, P], F32, tag="ga_flipped")
+            t_flipped = flipped.tile([P, PACK, P], F32, tag="t_flipped")
+            for target, source in (
+                (pwc_flipped, pwc_in[c][:, i, :]), (ga_flipped, ga[:]), (t_flipped, gapw[:]),
+            ):
+                for b in range(PACK):
+                    nc.tensor.transpose(target[:, b, :], source[:, b * P : (b + 1) * P], identity[:])
+            live[j] = {"pwc_flipped": pwc_flipped, "ga_flipped": ga_flipped, "t_flipped": t_flipped}
+
+        def scale_and_combine(j):
+            t = live[j]
+            h2 = work.tile([P, PACK, P], F32, tag="h2")
+            for b in range(PACK):
+                nc.scalar.activation(
+                    out=h2[:, b, :], in_=t["t_flipped"][:, b, :], func=ACT.Copy,
+                    scale=two_over_sigma2[:, b : b + 1],
+                )
+            minus_rowsum_ps = sums.tile([P, SUM_COLS], F32, tag="minus_rowsum_ps")
+            for b in range(PACK):
+                nc.tensor.matmul(
+                    minus_rowsum_ps[:], lhsT=h2[:, b, :], rhs=minus_ones[:],
+                    start=(b == 0), stop=(b == PACK - 1),
+                )
+            d_h2 = work.tile([P, 2, P, PACK], BF16, align_bytes=64, tag="d_h2")
+            nc.scalar.copy(out=d_h2[:, 1, :, :], in_=h2[:].rearrange("q b r -> q r b"))
+            second = work.tile([P, PACK, P], F32, tag="second")
+            for b in range(PACK):
+                nc.vector.scalar_tensor_tensor(
+                    out=second[:, b, :], in0=t["pwc_flipped"][:, b, :],
+                    scalar=one_over_wnorm[:, b : b + 1], in1=h2[:, b, :], op0=MULT, op1=MULT,
+                )
+            nc.vector.tensor_tensor(
+                out=d_h2[:, 0, :, :], in0=second[:].rearrange("q b r -> q r b"),
+                in1=t["ga_flipped"][:].rearrange("q b r -> q r b"), op=ADD,
+            )
+            live[j] = {"d_h2": d_h2, "minus_rowsum_ps": minus_rowsum_ps}
+
+        def quantise_and_multiply(j):
+            t = live[j]
+            minus_rowsum = work.tile([P, 1], F32, tag="minus_rowsum")
+            nc.scalar.copy(out=minus_rowsum[:], in_=t["minus_rowsum_ps"][:, 0:1])
+            codes = work.tile([P, 2 * P], U32, align_bytes=64, tag="codes")
+            scales = work.tile([P, 2 * P], U8, align_bytes=64, tag="scales")
+            nc.vector.quantize_mx(
+                out=codes[:].bitcast(E5M2_X4), scales=scales[:],
+                in_=t["d_h2"][:].rearrange("q s r b -> q (s r b)"),
+            )
+            acc = sums.tile([P, F_IN], F32, tag="acc")
+            nc.tensor.matmul_mx(
+                out=acc[:], lhsT=codes[:, 0:P].bitcast(E5M2_X4), lhsT_scale=scales[:, 0:P],
+                rhs=w_codes[:].bitcast(E4M3_X4), rhs_scale=w_scales[:], start=True, stop=False,
+            )
+            nc.tensor.matmul_mx(
+                out=acc[:], lhsT=codes[:, P : 2 * P].bitcast(E5M2_X4), lhsT_scale=scales[:, P : 2 * P],
+                rhs=c_codes[:].bitcast(E4M3_X4), rhs_scale=c_scales[:], start=False, stop=True,
+            )
+            live[j] = {"acc": acc, "minus_rowsum": minus_rowsum}
+
+        def finish(j):
+            c, i = divmod(j, CHUNK)
+            t = live.pop(j)
+            if i == 0:
+                live["result"] = results.tile([P, CHUNK, F_IN], F32, name="result")
+            result = live["result"]
+            nc.vector.scalar_tensor_tensor(
+                out=result[:, i, :], in0=x_in[c][:, i, :], scalar=t["minus_rowsum"][:],
+                in1=t["acc"][:], op0=MULT, op1=ADD,
+            )
+            if i == CHUNK - 1:
+                nc.sync.dma_start(
+                    out=by_token_tile(out)[:, c * CHUNK : (c + 1) * CHUNK, :], in_=result[:]
+                )
+
+        for step in range(TILES + 3):
+            if 0 <= step - 3:
+                finish(step - 3)
+            if 0 <= step - 2 < TILES:
+                quantise_and_multiply(step - 2)
+            if step < TILES:
+                products_and_transposes(step)
+            if 0 <= step - 1 < TILES:
+                scale_and_combine(step - 1)

@@ -22,6 +22,7 @@ TILES = TOKENS // P
 CHUNK = 2
 CHUNKS = TILES // CHUNK
 SUM_COLS = 64
+X_LAG = 2
 
 FLOPS = 2 * 2 * TOKENS * F_OUT * F_IN
 
@@ -38,6 +39,7 @@ def tile_orthogonallyattenuatedlinear_t_v_kernel(
         consts = stack.enter_context(tc.tile_pool(name="consts", bufs=1))
         inputs = stack.enter_context(tc.tile_pool(name="inputs", bufs=1))
         work = stack.enter_context(tc.tile_pool(name="work", bufs=3))
+        small = stack.enter_context(tc.tile_pool(name="small", bufs=4))
         results = stack.enter_context(tc.tile_pool(name="results", bufs=3))
         flipped = stack.enter_context(tc.psum_pool(name="flipped", bufs=2))
         sums = stack.enter_context(tc.psum_pool(name="sums", bufs=1))
@@ -49,22 +51,27 @@ def tile_orthogonallyattenuatedlinear_t_v_kernel(
         w_raw = consts.tile([P, PACK, F_IN], BF16)
         c_raw = consts.tile([P, PACK, F_IN], BF16)
         g_in, om_in, pw_in, pwc_in, x_in = [], [], [], [], []
-        for c in range(CHUNKS):
-            tiles_of_chunk = slice(c * CHUNK, (c + 1) * CHUNK)
-            for held, source, dtype, label in (
-                (g_in, grad_out, BF16, "g"),
-                (om_in, om, F32, "om"),
-                (pw_in, pw, F32, "pw"),
-                (pwc_in, pwc, F32, "pwc"),
-                (x_in, x, BF16, "x"),
-            ):
-                loaded = inputs.tile([P, CHUNK, F_OUT], dtype, name="%s%d" % (label, c))
-                nc.sync.dma_start(out=loaded[:], in_=by_token_tile(source)[:, tiles_of_chunk, :])
-                held.append(loaded)
-                if c == 0 and label == "om":
-                    nc.sync.dma_start(out=w_raw[:], in_=weights.rearrange("(b q) k -> q b k", q=P))
-                if c == 0 and label == "pwc":
-                    nc.sync.dma_start(out=c_raw[:], in_=center.rearrange("(b q) k -> q b k", q=P))
+
+        def load_chunk(held, source, dtype, label, c):
+            loaded = inputs.tile([P, CHUNK, F_OUT], dtype, name="%s%d" % (label, c))
+            nc.sync.dma_start(
+                out=loaded[:], in_=by_token_tile(source)[:, c * CHUNK : (c + 1) * CHUNK, :]
+            )
+            held.append(loaded)
+
+        for c in range(CHUNKS + X_LAG):
+            if c < CHUNKS:
+                load_chunk(g_in, grad_out, BF16, "g", c)
+                load_chunk(om_in, om, F32, "om", c)
+                load_chunk(pw_in, pw, F32, "pw", c)
+            if c == 0:
+                nc.sync.dma_start(out=w_raw[:], in_=weights.rearrange("(b q) k -> q b k", q=P))
+            if c < CHUNKS:
+                load_chunk(pwc_in, pwc, F32, "pwc", c)
+            if c == 0:
+                nc.sync.dma_start(out=c_raw[:], in_=center.rearrange("(b q) k -> q b k", q=P))
+            if c >= X_LAG:
+                load_chunk(x_in, x, BF16, "x", c - X_LAG)
 
         identity = consts.tile([P, P], F32)
         make_identity(nc, identity[:])
@@ -117,24 +124,31 @@ def tile_orthogonallyattenuatedlinear_t_v_kernel(
         c_codes, c_scales = quantise_matrix(c_raw, "c")
 
         live = {}
+        result_of_chunk = {}
 
-        def products_and_transposes(j):
+        def flip(source, label):
+            bank = flipped.tile([P, PACK, P], F32, name=label, tag=label)
+            for b in range(PACK):
+                nc.tensor.transpose(bank[:, b, :], source[:, b * P : (b + 1) * P], identity[:])
+            return bank
+
+        def products(j):
             c, i = divmod(j, CHUNK)
             ga = work.tile([P, F_OUT], F32, tag="ga")
             nc.gpsimd.tensor_tensor(out=ga[:], in0=g_in[c][:, i, :], in1=om_in[c][:, i, :], op=MULT)
             gapw = work.tile([P, F_OUT], F32, tag="gapw")
             nc.gpsimd.tensor_tensor(out=gapw[:], in0=ga[:], in1=pw_in[c][:, i, :], op=MULT)
-            pwc_flipped = flipped.tile([P, PACK, P], F32, tag="pwc_flipped")
-            ga_flipped = flipped.tile([P, PACK, P], F32, tag="ga_flipped")
-            t_flipped = flipped.tile([P, PACK, P], F32, tag="t_flipped")
-            for target, source in (
-                (pwc_flipped, pwc_in[c][:, i, :]), (ga_flipped, ga[:]), (t_flipped, gapw[:]),
-            ):
-                for b in range(PACK):
-                    nc.tensor.transpose(target[:, b, :], source[:, b * P : (b + 1) * P], identity[:])
-            live[j] = {"pwc_flipped": pwc_flipped, "ga_flipped": ga_flipped, "t_flipped": t_flipped}
+            live[j] = {"ga": ga, "gapw": gapw}
 
-        def scale_and_combine(j):
+        def flip_pwc_and_ga(j):
+            c, i = divmod(j, CHUNK)
+            live[j]["pwc_flipped"] = flip(pwc_in[c][:, i, :], "pwc_flipped")
+            live[j]["ga_flipped"] = flip(live[j]["ga"][:], "ga_flipped")
+
+        def flip_gapw(j):
+            live[j]["t_flipped"] = flip(live[j]["gapw"][:], "t_flipped")
+
+        def scale_h2(j):
             t = live[j]
             h2 = work.tile([P, PACK, P], F32, tag="h2")
             for b in range(PACK):
@@ -150,21 +164,26 @@ def tile_orthogonallyattenuatedlinear_t_v_kernel(
                 )
             d_h2 = work.tile([P, 2, P, PACK], BF16, align_bytes=64, tag="d_h2")
             nc.scalar.copy(out=d_h2[:, 1, :, :], in_=h2[:].rearrange("q b r -> q r b"))
+            t["h2"] = h2
+            t["d_h2"] = d_h2
+            t["minus_rowsum_ps"] = minus_rowsum_ps
+
+        def combine_d(j):
+            t = live[j]
             second = work.tile([P, PACK, P], F32, tag="second")
             for b in range(PACK):
                 nc.vector.scalar_tensor_tensor(
                     out=second[:, b, :], in0=t["pwc_flipped"][:, b, :],
-                    scalar=one_over_wnorm[:, b : b + 1], in1=h2[:, b, :], op0=MULT, op1=MULT,
+                    scalar=one_over_wnorm[:, b : b + 1], in1=t["h2"][:, b, :], op0=MULT, op1=MULT,
                 )
             nc.vector.tensor_tensor(
-                out=d_h2[:, 0, :, :], in0=second[:].rearrange("q b r -> q r b"),
+                out=t["d_h2"][:, 0, :, :], in0=second[:].rearrange("q b r -> q r b"),
                 in1=t["ga_flipped"][:].rearrange("q b r -> q r b"), op=ADD,
             )
-            live[j] = {"d_h2": d_h2, "minus_rowsum_ps": minus_rowsum_ps}
 
-        def quantise_and_multiply(j):
+        def quantise(j):
             t = live[j]
-            minus_rowsum = work.tile([P, 1], F32, tag="minus_rowsum")
+            minus_rowsum = small.tile([P, 1], F32, tag="minus_rowsum")
             nc.scalar.copy(out=minus_rowsum[:], in_=t["minus_rowsum_ps"][:, 0:1])
             codes = work.tile([P, 2 * P], U32, align_bytes=64, tag="codes")
             scales = work.tile([P, 2 * P], U8, align_bytes=64, tag="scales")
@@ -172,6 +191,13 @@ def tile_orthogonallyattenuatedlinear_t_v_kernel(
                 out=codes[:].bitcast(E5M2_X4), scales=scales[:],
                 in_=t["d_h2"][:].rearrange("q s r b -> q (s r b)"),
             )
+            t["minus_rowsum"] = minus_rowsum
+            t["codes"] = codes
+            t["scales"] = scales
+
+        def multiply(j):
+            t = live[j]
+            codes, scales = t["codes"], t["scales"]
             acc = sums.tile([P, F_IN], F32, tag="acc")
             nc.tensor.matmul_mx(
                 out=acc[:], lhsT=codes[:, 0:P].bitcast(E5M2_X4), lhsT_scale=scales[:, 0:P],
@@ -181,14 +207,14 @@ def tile_orthogonallyattenuatedlinear_t_v_kernel(
                 out=acc[:], lhsT=codes[:, P : 2 * P].bitcast(E5M2_X4), lhsT_scale=scales[:, P : 2 * P],
                 rhs=c_codes[:].bitcast(E4M3_X4), rhs_scale=c_scales[:], start=False, stop=True,
             )
-            live[j] = {"acc": acc, "minus_rowsum": minus_rowsum}
+            t["acc"] = acc
 
         def finish(j):
             c, i = divmod(j, CHUNK)
             t = live.pop(j)
             if i == 0:
-                live["result"] = results.tile([P, CHUNK, F_IN], F32, name="result")
-            result = live["result"]
+                result_of_chunk[c] = results.tile([P, CHUNK, F_IN], F32, name="result")
+            result = result_of_chunk[c]
             nc.vector.scalar_tensor_tensor(
                 out=result[:, i, :], in0=x_in[c][:, i, :], scalar=t["minus_rowsum"][:],
                 in1=t["acc"][:], op0=MULT, op1=ADD,
@@ -198,12 +224,23 @@ def tile_orthogonallyattenuatedlinear_t_v_kernel(
                     out=by_token_tile(out)[:, c * CHUNK : (c + 1) * CHUNK, :], in_=result[:]
                 )
 
-        for step in range(TILES + 3):
-            if 0 <= step - 3:
-                finish(step - 3)
-            if 0 <= step - 2 < TILES:
-                quantise_and_multiply(step - 2)
-            if step < TILES:
-                products_and_transposes(step)
-            if 0 <= step - 1 < TILES:
-                scale_and_combine(step - 1)
+        def in_range(j):
+            return 0 <= j < TILES
+
+        with tc.manual_schedule():
+            for step in range(TILES + 4):
+                if in_range(step - 4):
+                    finish(step - 4)
+                if in_range(step - 2):
+                    quantise(step - 2)
+                if in_range(step):
+                    products(step)
+                    flip_pwc_and_ga(step)
+                if in_range(step - 1):
+                    scale_h2(step - 1)
+                if in_range(step):
+                    flip_gapw(step)
+                if in_range(step - 1):
+                    combine_d(step - 1)
+                if in_range(step - 3):
+                    multiply(step - 3)

@@ -21,7 +21,6 @@ PACK = 4
 TILES = TOKENS // P
 CHUNK = 2
 CHUNKS = TILES // CHUNK
-SUM_COLS = 64
 X_LAG = 2
 
 FLOPS = 2 * 2 * TOKENS * F_OUT * F_IN
@@ -75,8 +74,6 @@ def tile_orthogonallyattenuatedlinear_t_v_kernel(
 
         identity = consts.tile([P, P], F32)
         make_identity(nc, identity[:])
-        minus_ones = consts.tile([P, SUM_COLS], F32)
-        nc.vector.memset(minus_ones[:], -1.0)
 
         warm = consts.tile([P, 1], F32)
         nc.vector.memset(warm[:], 1.0)
@@ -156,17 +153,14 @@ def tile_orthogonallyattenuatedlinear_t_v_kernel(
                     out=h2[:, b, :], in_=t["t_flipped"][:, b, :], func=ACT.Copy,
                     scale=two_over_sigma2[:, b : b + 1],
                 )
-            minus_rowsum_ps = sums.tile([P, SUM_COLS], F32, tag="minus_rowsum_ps")
+            h2_by_token = sums.tile([P, PACK, P], F32, tag="h2_by_token")
             for b in range(PACK):
-                nc.tensor.matmul(
-                    minus_rowsum_ps[:], lhsT=h2[:, b, :], rhs=minus_ones[:],
-                    start=(b == 0), stop=(b == PACK - 1),
-                )
+                nc.tensor.transpose(h2_by_token[:, b, :], h2[:, b, :], identity[:])
             d_h2 = work.tile([P, 2, P, PACK], BF16, align_bytes=64, tag="d_h2")
             nc.scalar.copy(out=d_h2[:, 1, :, :], in_=h2[:].rearrange("q b r -> q r b"))
             t["h2"] = h2
             t["d_h2"] = d_h2
-            t["minus_rowsum_ps"] = minus_rowsum_ps
+            t["h2_by_token"] = h2_by_token
 
         def combine_d(j):
             t = live[j]
@@ -184,7 +178,11 @@ def tile_orthogonallyattenuatedlinear_t_v_kernel(
         def quantise(j):
             t = live[j]
             minus_rowsum = small.tile([P, 1], F32, tag="minus_rowsum")
-            nc.scalar.copy(out=minus_rowsum[:], in_=t["minus_rowsum_ps"][:, 0:1])
+            unread = work.tile([P, PACK, P], BF16, tag="unread")
+            nc.scalar.activation(
+                out=unread[:], in_=t["h2_by_token"][:], func=ACT.Copy, scale=-1.0,
+                accum_out=minus_rowsum[:],
+            )
             codes = work.tile([P, 2 * P], U32, align_bytes=64, tag="codes")
             scales = work.tile([P, 2 * P], U8, align_bytes=64, tag="scales")
             nc.vector.quantize_mx(

@@ -122,6 +122,7 @@ def tile_orthogonallyattenuatedlinear_t_v_kernel(
 
         live = {}
         result_of_chunk = {}
+        ga_of_chunk = {}
 
         def flip(source, label):
             bank = flipped.tile([P, PACK, P], F32, name=label, tag=label)
@@ -131,16 +132,18 @@ def tile_orthogonallyattenuatedlinear_t_v_kernel(
 
         def products(j):
             c, i = divmod(j, CHUNK)
-            ga = work.tile([P, F_OUT], F32, tag="ga")
-            nc.gpsimd.tensor_tensor(out=ga[:], in0=g_in[c][:, i, :], in1=om_in[c][:, i, :], op=MULT)
+            if i == 0:
+                ga_of_chunk[c] = work.tile([P, CHUNK, F_OUT], F32, name="ga")
+                nc.gpsimd.tensor_tensor(out=ga_of_chunk[c][:], in0=g_in[c][:], in1=om_in[c][:], op=MULT)
+            ga = ga_of_chunk[c][:, i, :]
             gapw = work.tile([P, F_OUT], F32, tag="gapw")
-            nc.gpsimd.tensor_tensor(out=gapw[:], in0=ga[:], in1=pw_in[c][:, i, :], op=MULT)
+            nc.gpsimd.tensor_tensor(out=gapw[:], in0=ga, in1=pw_in[c][:, i, :], op=MULT)
             live[j] = {"ga": ga, "gapw": gapw}
 
         def flip_pwc_and_ga(j):
             c, i = divmod(j, CHUNK)
             live[j]["pwc_flipped"] = flip(pwc_in[c][:, i, :], "pwc_flipped")
-            live[j]["ga_flipped"] = flip(live[j]["ga"][:], "ga_flipped")
+            live[j]["ga_flipped"] = flip(live[j]["ga"], "ga_flipped")
 
         def flip_gapw(j):
             live[j]["t_flipped"] = flip(live[j]["gapw"][:], "t_flipped")
@@ -153,9 +156,12 @@ def tile_orthogonallyattenuatedlinear_t_v_kernel(
                     out=h2[:, b, :], in_=t["t_flipped"][:, b, :], func=ACT.Copy,
                     scale=two_over_sigma2[:, b : b + 1],
                 )
-            h2_by_token = sums.tile([P, PACK, P], F32, tag="h2_by_token")
+            h2_by_token = sums.tile([P, P], F32, tag="h2_by_token")
             for b in range(PACK):
-                nc.tensor.transpose(h2_by_token[:, b, :], h2[:, b, :], identity[:])
+                nc.tensor.matmul(
+                    h2_by_token[:], lhsT=h2[:, b, :], rhs=identity[:], is_transpose=True,
+                    start=(b == 0), stop=(b == PACK - 1),
+                )
             d_h2 = work.tile([P, 2, P, PACK], BF16, align_bytes=64, tag="d_h2")
             nc.scalar.copy(out=d_h2[:, 1, :, :], in_=h2[:].rearrange("q b r -> q r b"))
             t["h2"] = h2
@@ -178,7 +184,7 @@ def tile_orthogonallyattenuatedlinear_t_v_kernel(
         def quantise(j):
             t = live[j]
             minus_rowsum = small.tile([P, 1], F32, tag="minus_rowsum")
-            unread = work.tile([P, PACK, P], BF16, tag="unread")
+            unread = work.tile([P, P], BF16, tag="unread")
             nc.scalar.activation(
                 out=unread[:], in_=t["h2_by_token"][:], func=ACT.Copy, scale=-1.0,
                 accum_out=minus_rowsum[:],

@@ -20,7 +20,7 @@ F_IN = 512
 PACK = 4
 TILES = TOKENS // P
 CHUNK = 2
-CHUNKS = TILES // CHUNK
+LOAD_SPANS = (1, 1, 2, 2, 2, 2, 2, 2, 2)
 X_LAG = 2
 
 FLOPS = 2 * 2 * TOKENS * F_OUT * F_IN
@@ -37,11 +37,13 @@ def tile_orthogonallyattenuatedlinear_t_v_kernel(
     with ExitStack() as stack:
         consts = stack.enter_context(tc.tile_pool(name="consts", bufs=1))
         inputs = stack.enter_context(tc.tile_pool(name="inputs", bufs=1))
-        work = stack.enter_context(tc.tile_pool(name="work", bufs=3))
+        work = stack.enter_context(tc.tile_pool(name="work", bufs=2))
+        deep = stack.enter_context(tc.tile_pool(name="deep", bufs=3))
         small = stack.enter_context(tc.tile_pool(name="small", bufs=4))
-        results = stack.enter_context(tc.tile_pool(name="results", bufs=3))
+        results = stack.enter_context(tc.tile_pool(name="results", bufs=TILES // CHUNK))
         flipped = stack.enter_context(tc.psum_pool(name="flipped", bufs=2))
         sums = stack.enter_context(tc.psum_pool(name="sums", bufs=1))
+        stack.enter_context(tc.manual_schedule())
 
         sigma_rows_bf = consts.tile([P, P], BF16)
         nc.vector.memset(sigma_rows_bf[:], 0.0)
@@ -49,28 +51,30 @@ def tile_orthogonallyattenuatedlinear_t_v_kernel(
 
         w_raw = consts.tile([P, PACK, F_IN], BF16)
         c_raw = consts.tile([P, PACK, F_IN], BF16)
-        g_in, om_in, pw_in, pwc_in, x_in = [], [], [], [], []
+        nc.sync.dma_start(out=w_raw[:], in_=weights.rearrange("(b q) k -> q b k", q=P))
 
-        def load_chunk(held, source, dtype, label, c):
-            loaded = inputs.tile([P, CHUNK, F_OUT], dtype, name="%s%d" % (label, c))
-            nc.sync.dma_start(
-                out=loaded[:], in_=by_token_tile(source)[:, c * CHUNK : (c + 1) * CHUNK, :]
-            )
-            held.append(loaded)
+        spans = []
+        for count in LOAD_SPANS:
+            spans.append((sum(LOAD_SPANS[: len(spans)]), count))
+        g_in, om_in, pw_in, pwc_in, x_in = {}, {}, {}, {}, {}
 
-        for c in range(CHUNKS + X_LAG):
-            if c < CHUNKS:
-                load_chunk(g_in, grad_out, BF16, "g", c)
-                load_chunk(om_in, om, F32, "om", c)
-                load_chunk(pw_in, pw, F32, "pw", c)
-            if c == 0:
-                nc.sync.dma_start(out=w_raw[:], in_=weights.rearrange("(b q) k -> q b k", q=P))
-            if c < CHUNKS:
-                load_chunk(pwc_in, pwc, F32, "pwc", c)
-            if c == 0:
+        def load_span(held, source, dtype, label, span):
+            first, count = span
+            loaded = inputs.tile([P, count, F_OUT], dtype, name="%s%d" % (label, first))
+            nc.sync.dma_start(out=loaded[:], in_=by_token_tile(source)[:, first : first + count, :])
+            for i in range(count):
+                held[first + i] = loaded[:, i, :]
+
+        for s in range(len(spans) + X_LAG):
+            if s < len(spans):
+                load_span(g_in, grad_out, BF16, "g", spans[s])
+                load_span(om_in, om, F32, "om", spans[s])
+                load_span(pw_in, pw, F32, "pw", spans[s])
+                load_span(pwc_in, pwc, F32, "pwc", spans[s])
+            if s == 0:
                 nc.sync.dma_start(out=c_raw[:], in_=center.rearrange("(b q) k -> q b k", q=P))
-            if c >= X_LAG:
-                load_chunk(x_in, x, BF16, "x", c - X_LAG)
+            if s >= X_LAG:
+                load_span(x_in, x, BF16, "x", spans[s - X_LAG])
 
         identity = consts.tile([P, P], F32)
         make_identity(nc, identity[:])
@@ -81,7 +85,7 @@ def tile_orthogonallyattenuatedlinear_t_v_kernel(
 
         sigma_rows = consts.tile([P, P], F32)
         nc.vector.tensor_copy(out=sigma_rows[:], in_=sigma_rows_bf[:])
-        sigma_flipped = flipped.tile([P, PACK, P], F32, tag="t_flipped")
+        sigma_flipped = flipped.tile([P, PACK, P], F32, tag="pw_flipped")
         nc.tensor.transpose(sigma_flipped[:, 0, :], sigma_rows[:], identity[:])
         sigma_cols = consts.tile([P, PACK], F32)
         nc.vector.tensor_copy(out=sigma_cols[:], in_=sigma_flipped[:, 0, 0:PACK])
@@ -91,20 +95,6 @@ def tile_orthogonallyattenuatedlinear_t_v_kernel(
         )
         two_over_sigma2 = consts.tile([P, PACK], F32)
         nc.vector.reciprocal(out=two_over_sigma2[:], in_=half_sigma2[:])
-
-        squares = consts.tile([P, PACK, F_IN], BF16)
-        sum_squares = consts.tile([P, PACK], F32)
-        for b in range(PACK):
-            nc.scalar.activation(
-                out=squares[:, b, :], in_=w_raw[:, b, :], func=ACT.Square,
-                accum_out=sum_squares[:, b : b + 1],
-            )
-        wnorm = consts.tile([P, PACK], F32)
-        nc.scalar.sqrt(out=wnorm[:], in_=sum_squares[:])
-        wnorm_floor = consts.tile([P, PACK], F32)
-        nc.vector.tensor_scalar_max(out=wnorm_floor[:], in0=wnorm[:], scalar1=1e-12)
-        one_over_wnorm = consts.tile([P, PACK], F32)
-        nc.vector.reciprocal(out=one_over_wnorm[:], in_=wnorm_floor[:])
 
         def quantise_matrix(raw, label):
             grouped = consts.tile([P, F_IN, PACK], BF16, align_bytes=64, name=label + "_grouped")
@@ -117,12 +107,34 @@ def tile_orthogonallyattenuatedlinear_t_v_kernel(
             )
             return codes, scales
 
+        squares = consts.tile([P, PACK, F_IN], BF16)
+        sum_squares = consts.tile([P, PACK], F32)
+        for b in range(PACK):
+            nc.scalar.activation(
+                out=squares[:, b, :], in_=w_raw[:, b, :], func=ACT.Square,
+                accum_out=sum_squares[:, b : b + 1],
+            )
+        wnorm = consts.tile([P, PACK], F32)
+        nc.scalar.sqrt(out=wnorm[:], in_=sum_squares[:])
+
         w_codes, w_scales = quantise_matrix(w_raw, "w")
+
+        wnorm_floor = consts.tile([P, PACK], F32)
+        nc.vector.tensor_scalar_max(out=wnorm_floor[:], in0=wnorm[:], scalar1=1e-12)
+        one_over_wnorm = consts.tile([P, PACK], F32)
+        nc.vector.reciprocal(out=one_over_wnorm[:], in_=wnorm_floor[:])
+        two_over_sigma2_wnorm = consts.tile([P, PACK], F32)
+        nc.vector.tensor_tensor(
+            out=two_over_sigma2_wnorm[:], in0=two_over_sigma2[:], in1=one_over_wnorm[:], op=MULT
+        )
+
         c_codes, c_scales = quantise_matrix(c_raw, "c")
 
         live = {}
         result_of_chunk = {}
-        ga_of_chunk = {}
+
+        def state(j):
+            return live.setdefault(j, {})
 
         def flip(source, label):
             bank = flipped.tile([P, PACK, P], F32, name=label, tag=label)
@@ -130,77 +142,94 @@ def tile_orthogonallyattenuatedlinear_t_v_kernel(
                 nc.tensor.transpose(bank[:, b, :], source[:, b * P : (b + 1) * P], identity[:])
             return bank
 
-        def products(j):
-            c, i = divmod(j, CHUNK)
-            if i == 0:
-                ga_of_chunk[c] = work.tile([P, CHUNK, F_OUT], F32, name="ga")
-                nc.gpsimd.tensor_tensor(out=ga_of_chunk[c][:], in0=g_in[c][:], in1=om_in[c][:], op=MULT)
-            ga = ga_of_chunk[c][:, i, :]
-            gapw = work.tile([P, F_OUT], F32, tag="gapw")
-            nc.gpsimd.tensor_tensor(out=gapw[:], in0=ga, in1=pw_in[c][:, i, :], op=MULT)
-            live[j] = {"ga": ga, "gapw": gapw}
+        def make_ga(j):
+            ga = work.tile([P, F_OUT], F32, tag="ga")
+            nc.gpsimd.tensor_tensor(out=ga[:], in0=g_in[j], in1=om_in[j], op=MULT)
+            state(j)["ga"] = ga
 
-        def flip_pwc_and_ga(j):
-            c, i = divmod(j, CHUNK)
-            live[j]["pwc_flipped"] = flip(pwc_in[c][:, i, :], "pwc_flipped")
-            live[j]["ga_flipped"] = flip(live[j]["ga"], "ga_flipped")
+        def flip_pw(j):
+            state(j)["pw_flipped"] = flip(pw_in[j], "pw_flipped")
 
-        def flip_gapw(j):
-            live[j]["t_flipped"] = flip(live[j]["gapw"][:], "t_flipped")
+        def flip_pwc(j):
+            state(j)["pwc_flipped"] = flip(pwc_in[j], "pwc_flipped")
 
-        def scale_h2(j):
-            t = live[j]
-            h2 = work.tile([P, PACK, P], F32, tag="h2")
+        def flip_ga(j):
+            state(j)["ga_flipped"] = flip(state(j)["ga"][:], "ga_flipped")
+
+        def scale_pw(j):
+            t = state(j)
+            pw_s = deep.tile([P, PACK, P], F32, tag="pw_s")
+            pw_k = deep.tile([P, PACK, P], F32, tag="pw_k")
             for b in range(PACK):
                 nc.scalar.activation(
-                    out=h2[:, b, :], in_=t["t_flipped"][:, b, :], func=ACT.Copy,
+                    out=pw_s[:, b, :], in_=t["pw_flipped"][:, b, :], func=ACT.Copy,
                     scale=two_over_sigma2[:, b : b + 1],
                 )
+            for b in range(PACK):
+                nc.scalar.activation(
+                    out=pw_k[:, b, :], in_=t["pw_flipped"][:, b, :], func=ACT.Copy,
+                    scale=two_over_sigma2_wnorm[:, b : b + 1],
+                )
+            t["pw_s"] = pw_s
+            t["pw_k"] = pw_k
+
+        def make_pp(j):
+            t = state(j)
+            pp = work.tile([P, PACK, P], F32, tag="pp")
+            nc.vector.tensor_tensor(out=pp[:], in0=t["pw_k"][:], in1=t["pwc_flipped"][:], op=MULT)
+            t["pp"] = pp
+
+        def make_h2(j):
+            t = state(j)
+            h2 = work.tile([P, PACK, P], F32, tag="h2")
+            nc.vector.tensor_tensor(out=h2[:], in0=t["pw_s"][:], in1=t["ga_flipped"][:], op=MULT)
+            t["h2"] = h2
+            t["d_h2"] = deep.tile([P, 2, P, PACK], BF16, align_bytes=64, name="d_h2", tag="d_h2")
+
+        def cast_h2(j):
+            t = state(j)
+            nc.scalar.copy(out=t["d_h2"][:, 1, :, :], in_=t["h2"][:].rearrange("q b r -> q r b"))
+
+        def back(j):
+            t = state(j)
             h2_by_token = sums.tile([P, P], F32, tag="h2_by_token")
             for b in range(PACK):
                 nc.tensor.matmul(
-                    h2_by_token[:], lhsT=h2[:, b, :], rhs=identity[:], is_transpose=True,
+                    h2_by_token[:], lhsT=t["h2"][:, b, :], rhs=identity[:], is_transpose=True,
                     start=(b == 0), stop=(b == PACK - 1),
                 )
-            d_h2 = work.tile([P, 2, P, PACK], BF16, align_bytes=64, tag="d_h2")
-            nc.scalar.copy(out=d_h2[:, 1, :, :], in_=h2[:].rearrange("q b r -> q r b"))
-            t["h2"] = h2
-            t["d_h2"] = d_h2
             t["h2_by_token"] = h2_by_token
 
-        def combine_d(j):
-            t = live[j]
-            second = work.tile([P, PACK, P], F32, tag="second")
-            for b in range(PACK):
-                nc.vector.scalar_tensor_tensor(
-                    out=second[:, b, :], in0=t["pwc_flipped"][:, b, :],
-                    scalar=one_over_wnorm[:, b : b + 1], in1=t["h2"][:, b, :], op0=MULT, op1=MULT,
-                )
-            nc.vector.tensor_tensor(
-                out=t["d_h2"][:, 0, :, :], in0=second[:].rearrange("q b r -> q r b"),
-                in1=t["ga_flipped"][:].rearrange("q b r -> q r b"), op=ADD,
+        def make_d(j):
+            t = state(j)
+            nc.vector.scalar_tensor_tensor(
+                out=t["d_h2"][:, 0, :, :], in0=t["pp"][:].rearrange("q b r -> q r b"), scalar=1.0,
+                in1=t["ga_flipped"][:].rearrange("q b r -> q r b"), op0=ADD, op1=MULT,
             )
 
-        def quantise(j):
-            t = live[j]
+        def rowsum(j):
+            t = state(j)
             minus_rowsum = small.tile([P, 1], F32, tag="minus_rowsum")
             unread = work.tile([P, P], BF16, tag="unread")
             nc.scalar.activation(
                 out=unread[:], in_=t["h2_by_token"][:], func=ACT.Copy, scale=-1.0,
                 accum_out=minus_rowsum[:],
             )
+            t["minus_rowsum"] = minus_rowsum
+
+        def quantise(j):
+            t = state(j)
             codes = work.tile([P, 2 * P], U32, align_bytes=64, tag="codes")
             scales = work.tile([P, 2 * P], U8, align_bytes=64, tag="scales")
             nc.vector.quantize_mx(
                 out=codes[:].bitcast(E5M2_X4), scales=scales[:],
                 in_=t["d_h2"][:].rearrange("q s r b -> q (s r b)"),
             )
-            t["minus_rowsum"] = minus_rowsum
             t["codes"] = codes
             t["scales"] = scales
 
         def multiply(j):
-            t = live[j]
+            t = state(j)
             codes, scales = t["codes"], t["scales"]
             acc = sums.tile([P, F_IN], F32, tag="acc")
             nc.tensor.matmul_mx(
@@ -220,7 +249,7 @@ def tile_orthogonallyattenuatedlinear_t_v_kernel(
                 result_of_chunk[c] = results.tile([P, CHUNK, F_IN], F32, name="result")
             result = result_of_chunk[c]
             nc.vector.scalar_tensor_tensor(
-                out=result[:, i, :], in0=x_in[c][:, i, :], scalar=t["minus_rowsum"][:],
+                out=result[:, i, :], in0=x_in[j], scalar=t["minus_rowsum"][:],
                 in1=t["acc"][:], op0=MULT, op1=ADD,
             )
             if i == CHUNK - 1:
@@ -231,20 +260,29 @@ def tile_orthogonallyattenuatedlinear_t_v_kernel(
         def in_range(j):
             return 0 <= j < TILES
 
-        with tc.manual_schedule():
-            for step in range(TILES + 4):
-                if in_range(step - 4):
-                    finish(step - 4)
-                if in_range(step - 2):
-                    quantise(step - 2)
-                if in_range(step):
-                    products(step)
-                    flip_pwc_and_ga(step)
-                if in_range(step - 1):
-                    scale_h2(step - 1)
-                if in_range(step):
-                    flip_gapw(step)
-                if in_range(step - 1):
-                    combine_d(step - 1)
-                if in_range(step - 3):
-                    multiply(step - 3)
+        for c in range(-3, TILES + 2):
+            if in_range(c - 1):
+                quantise(c - 1)
+            if in_range(c + 2):
+                flip_pw(c + 2)
+            if in_range(c + 1):
+                flip_ga(c + 1)
+            if in_range(c + 3):
+                make_ga(c + 3)
+            if in_range(c - 1):
+                multiply(c - 1)
+            if in_range(c):
+                make_h2(c)
+            if in_range(c + 2):
+                scale_pw(c + 2)
+            if in_range(c + 1):
+                make_pp(c + 1)
+            if in_range(c + 2):
+                flip_pwc(c + 2)
+            if in_range(c):
+                cast_h2(c)
+                back(c)
+                make_d(c)
+                rowsum(c)
+            if in_range(c - 1):
+                finish(c - 1)

@@ -20,7 +20,6 @@ F_IN = 512
 PACK = 4
 TILES = TOKENS // P
 CHUNK = 2
-LOAD_SPANS = (1, 1, 2, 2, 2, 2, 2, 2, 2)
 X_LAG = 2
 
 FLOPS = 2 * 2 * TOKENS * F_OUT * F_IN
@@ -52,29 +51,23 @@ def tile_orthogonallyattenuatedlinear_t_v_kernel(
         w_raw = consts.tile([P, PACK, F_IN], BF16)
         c_raw = consts.tile([P, PACK, F_IN], BF16)
         nc.sync.dma_start(out=w_raw[:], in_=weights.rearrange("(b q) k -> q b k", q=P))
+        nc.sync.dma_start(out=c_raw[:], in_=center.rearrange("(b q) k -> q b k", q=P))
 
-        spans = []
-        for count in LOAD_SPANS:
-            spans.append((sum(LOAD_SPANS[: len(spans)]), count))
         g_in, om_in, pw_in, pwc_in, x_in = {}, {}, {}, {}, {}
 
-        def load_span(held, source, dtype, label, span):
-            first, count = span
-            loaded = inputs.tile([P, count, F_OUT], dtype, name="%s%d" % (label, first))
-            nc.sync.dma_start(out=loaded[:], in_=by_token_tile(source)[:, first : first + count, :])
-            for i in range(count):
-                held[first + i] = loaded[:, i, :]
+        def load_tile(held, source, dtype, label, j):
+            loaded = inputs.tile([P, F_OUT], dtype, name="%s%d" % (label, j))
+            nc.sync.dma_start(out=loaded[:], in_=by_token_tile(source)[:, j, :])
+            held[j] = loaded[:]
 
-        for s in range(len(spans) + X_LAG):
-            if s < len(spans):
-                load_span(g_in, grad_out, BF16, "g", spans[s])
-                load_span(om_in, om, F32, "om", spans[s])
-                load_span(pw_in, pw, F32, "pw", spans[s])
-                load_span(pwc_in, pwc, F32, "pwc", spans[s])
-            if s == 0:
-                nc.sync.dma_start(out=c_raw[:], in_=center.rearrange("(b q) k -> q b k", q=P))
-            if s >= X_LAG:
-                load_span(x_in, x, BF16, "x", spans[s - X_LAG])
+        for j in range(TILES + X_LAG):
+            if j < TILES:
+                load_tile(pw_in, pw, F32, "pw", j)
+                load_tile(g_in, grad_out, BF16, "g", j)
+                load_tile(om_in, om, F32, "om", j)
+                load_tile(pwc_in, pwc, F32, "pwc", j)
+            if j >= X_LAG:
+                load_tile(x_in, x, BF16, "x", j - X_LAG)
 
         identity = consts.tile([P, P], F32)
         make_identity(nc, identity[:])
@@ -96,9 +89,7 @@ def tile_orthogonallyattenuatedlinear_t_v_kernel(
         two_over_sigma2 = consts.tile([P, PACK], F32)
         nc.vector.reciprocal(out=two_over_sigma2[:], in_=half_sigma2[:])
 
-        def quantise_matrix(raw, label):
-            grouped = consts.tile([P, F_IN, PACK], BF16, align_bytes=64, name=label + "_grouped")
-            nc.vector.tensor_copy(out=grouped[:], in_=raw[:].rearrange("q b k -> q k b"))
+        def quantise_matrix(grouped, label):
             codes = consts.tile([P, F_IN], U32, align_bytes=64, name=label + "_codes")
             scales = consts.tile([P, F_IN], U8, align_bytes=64, name=label + "_scales")
             nc.vector.quantize_mx(
@@ -117,20 +108,17 @@ def tile_orthogonallyattenuatedlinear_t_v_kernel(
         wnorm = consts.tile([P, PACK], F32)
         nc.scalar.sqrt(out=wnorm[:], in_=sum_squares[:])
 
-        w_codes, w_scales = quantise_matrix(w_raw, "w")
-
-        wnorm_floor = consts.tile([P, PACK], F32)
-        nc.vector.tensor_scalar_max(out=wnorm_floor[:], in0=wnorm[:], scalar1=1e-12)
-        one_over_wnorm = consts.tile([P, PACK], F32)
-        nc.vector.reciprocal(out=one_over_wnorm[:], in_=wnorm_floor[:])
-        two_over_sigma2_wnorm = consts.tile([P, PACK], F32)
-        nc.vector.tensor_tensor(
-            out=two_over_sigma2_wnorm[:], in0=two_over_sigma2[:], in1=one_over_wnorm[:], op=MULT
+        w_grouped = consts.tile([P, F_IN, PACK], BF16, align_bytes=64)
+        nc.vector.tensor_copy(out=w_grouped[:], in_=w_raw[:].rearrange("q b k -> q k b"))
+        c_grouped = consts.tile([P, F_IN, PACK], BF16, align_bytes=64)
+        nc.gpsimd.tensor_scalar(
+            out=c_grouped[:], in0=c_raw[:].rearrange("q b k -> q k b"), scalar1=1.0, scalar2=0.0,
+            op0=MULT, op1=ADD,
         )
-
-        c_codes, c_scales = quantise_matrix(c_raw, "c")
+        w_codes, w_scales = quantise_matrix(w_grouped, "w")
 
         live = {}
+        center_mx = []
         result_of_chunk = {}
 
         def state(j):
@@ -144,7 +132,8 @@ def tile_orthogonallyattenuatedlinear_t_v_kernel(
 
         def make_ga(j):
             ga = work.tile([P, F_OUT], F32, tag="ga")
-            nc.gpsimd.tensor_tensor(out=ga[:], in0=g_in[j], in1=om_in[j], op=MULT)
+            engine = nc.vector if j == 0 else nc.gpsimd
+            engine.tensor_tensor(out=ga[:], in0=g_in[j], in1=om_in[j], op=MULT)
             state(j)["ga"] = ga
 
         def flip_pw(j):
@@ -156,27 +145,35 @@ def tile_orthogonallyattenuatedlinear_t_v_kernel(
         def flip_ga(j):
             state(j)["ga_flipped"] = flip(state(j)["ga"][:], "ga_flipped")
 
-        def scale_pw(j):
+        def scaled_copy(source, factors, label):
+            scaled = deep.tile([P, PACK, P], F32, name=label, tag=label)
+            for b in range(PACK):
+                nc.scalar.activation(
+                    out=scaled[:, b, :], in_=source[:, b, :], func=ACT.Copy, scale=factors[:, b : b + 1]
+                )
+            return scaled
+
+        def pp_on_gpsimd(j):
+            return j % 2 == 1 and j > 1
+
+        def scale_s(j):
             t = state(j)
-            pw_s = deep.tile([P, PACK, P], F32, tag="pw_s")
-            pw_k = deep.tile([P, PACK, P], F32, tag="pw_k")
-            for b in range(PACK):
-                nc.scalar.activation(
-                    out=pw_s[:, b, :], in_=t["pw_flipped"][:, b, :], func=ACT.Copy,
-                    scale=two_over_sigma2[:, b : b + 1],
-                )
-            for b in range(PACK):
-                nc.scalar.activation(
-                    out=pw_k[:, b, :], in_=t["pw_flipped"][:, b, :], func=ACT.Copy,
-                    scale=two_over_sigma2_wnorm[:, b : b + 1],
-                )
-            t["pw_s"] = pw_s
-            t["pw_k"] = pw_k
+            t["pw_s"] = scaled_copy(t["pw_flipped"], two_over_sigma2, "pw_s")
+
+        def scale_k(j):
+            t = state(j)
+            if pp_on_gpsimd(j):
+                t["other"] = scaled_copy(t["pwc_flipped"], one_over_wnorm, "other")
+            else:
+                t["other"] = scaled_copy(t["pw_flipped"], two_over_sigma2_wnorm, "other")
 
         def make_pp(j):
             t = state(j)
-            pp = work.tile([P, PACK, P], F32, tag="pp")
-            nc.vector.tensor_tensor(out=pp[:], in0=t["pw_k"][:], in1=t["pwc_flipped"][:], op=MULT)
+            pp = deep.tile([P, PACK, P], F32, tag="pp")
+            if pp_on_gpsimd(j):
+                nc.gpsimd.tensor_tensor(out=pp[:], in0=t["pw_s"][:], in1=t["other"][:], op=MULT)
+            else:
+                nc.vector.tensor_tensor(out=pp[:], in0=t["other"][:], in1=t["pwc_flipped"][:], op=MULT)
             t["pp"] = pp
 
         def make_h2(j):
@@ -238,7 +235,7 @@ def tile_orthogonallyattenuatedlinear_t_v_kernel(
             )
             nc.tensor.matmul_mx(
                 out=acc[:], lhsT=codes[:, P : 2 * P].bitcast(E5M2_X4), lhsT_scale=scales[:, P : 2 * P],
-                rhs=c_codes[:].bitcast(E4M3_X4), rhs_scale=c_scales[:], start=False, stop=True,
+                rhs=center_mx[0][:].bitcast(E4M3_X4), rhs_scale=center_mx[1][:], start=False, stop=True,
             )
             t["acc"] = acc
 
@@ -252,13 +249,26 @@ def tile_orthogonallyattenuatedlinear_t_v_kernel(
                 out=result[:, i, :], in0=x_in[j], scalar=t["minus_rowsum"][:],
                 in1=t["acc"][:], op0=MULT, op1=ADD,
             )
-            if i == CHUNK - 1:
+            if c == TILES // CHUNK - 1:
+                nc.sync.dma_start(out=by_token_tile(out)[:, j, :], in_=result[:, i, :])
+            elif i == CHUNK - 1:
                 nc.sync.dma_start(
                     out=by_token_tile(out)[:, c * CHUNK : (c + 1) * CHUNK, :], in_=result[:]
                 )
 
         def in_range(j):
             return 0 <= j < TILES
+
+        make_ga(0)
+
+        wnorm_floor = consts.tile([P, PACK], F32)
+        nc.vector.tensor_scalar_max(out=wnorm_floor[:], in0=wnorm[:], scalar1=1e-12)
+        one_over_wnorm = consts.tile([P, PACK], F32)
+        nc.vector.reciprocal(out=one_over_wnorm[:], in_=wnorm_floor[:])
+        two_over_sigma2_wnorm = consts.tile([P, PACK], F32)
+        nc.vector.tensor_tensor(
+            out=two_over_sigma2_wnorm[:], in0=two_over_sigma2[:], in1=one_over_wnorm[:], op=MULT
+        )
 
         for c in range(-3, TILES + 2):
             if in_range(c - 1):
@@ -267,22 +277,28 @@ def tile_orthogonallyattenuatedlinear_t_v_kernel(
                 flip_pw(c + 2)
             if in_range(c + 1):
                 flip_ga(c + 1)
-            if in_range(c + 3):
+            if in_range(c + 3) and c + 3 > 0:
                 make_ga(c + 3)
             if in_range(c - 1):
                 multiply(c - 1)
             if in_range(c):
                 make_h2(c)
             if in_range(c + 2):
-                scale_pw(c + 2)
-            if in_range(c + 1):
-                make_pp(c + 1)
-            if in_range(c + 2):
+                scale_s(c + 2)
                 flip_pwc(c + 2)
+            if in_range(c + 1) and not pp_on_gpsimd(c + 1):
+                make_pp(c + 1)
             if in_range(c):
                 cast_h2(c)
+            if in_range(c + 2):
+                scale_k(c + 2)
+                if pp_on_gpsimd(c + 2):
+                    make_pp(c + 2)
+            if in_range(c):
                 back(c)
                 make_d(c)
                 rowsum(c)
+            if c == 0:
+                center_mx.extend(quantise_matrix(c_grouped, "c"))
             if in_range(c - 1):
                 finish(c - 1)

@@ -51,7 +51,6 @@ def tile_orthogonallyattenuatedlinear_t_v_kernel(
         w_raw = consts.tile([P, PACK, F_IN], BF16)
         c_raw = consts.tile([P, PACK, F_IN], BF16)
         nc.sync.dma_start(out=w_raw[:], in_=weights.rearrange("(b q) k -> q b k", q=P))
-        nc.sync.dma_start(out=c_raw[:], in_=center.rearrange("(b q) k -> q b k", q=P))
 
         g_in, om_in, pw_in, pwc_in, x_in = {}, {}, {}, {}, {}
 
@@ -66,6 +65,8 @@ def tile_orthogonallyattenuatedlinear_t_v_kernel(
                 load_tile(g_in, grad_out, BF16, "g", j)
                 load_tile(om_in, om, F32, "om", j)
                 load_tile(pwc_in, pwc, F32, "pwc", j)
+            if j == 0:
+                nc.sync.dma_start(out=c_raw[:], in_=center.rearrange("(b q) k -> q b k", q=P))
             if j >= X_LAG:
                 load_tile(x_in, x, BF16, "x", j - X_LAG)
 
@@ -110,11 +111,6 @@ def tile_orthogonallyattenuatedlinear_t_v_kernel(
 
         w_grouped = consts.tile([P, F_IN, PACK], BF16, align_bytes=64)
         nc.vector.tensor_copy(out=w_grouped[:], in_=w_raw[:].rearrange("q b k -> q k b"))
-        c_grouped = consts.tile([P, F_IN, PACK], BF16, align_bytes=64)
-        nc.gpsimd.tensor_scalar(
-            out=c_grouped[:], in0=c_raw[:].rearrange("q b k -> q k b"), scalar1=1.0, scalar2=0.0,
-            op0=MULT, op1=ADD,
-        )
         w_codes, w_scales = quantise_matrix(w_grouped, "w")
 
         live = {}
@@ -269,6 +265,9 @@ def tile_orthogonallyattenuatedlinear_t_v_kernel(
         nc.vector.tensor_tensor(
             out=two_over_sigma2_wnorm[:], in0=two_over_sigma2[:], in1=one_over_wnorm[:], op=MULT
         )
+
+        c_grouped = consts.tile([P, F_IN, PACK], BF16, align_bytes=64)
+        nc.vector.tensor_copy(out=c_grouped[:], in_=c_raw[:].rearrange("q b k -> q k b"))
 
         for c in range(-3, TILES + 2):
             if in_range(c - 1):

@@ -21,6 +21,7 @@ PACK = 4
 TILES = TOKENS // P
 CHUNK = 2
 X_LAG = 2
+GPSIMD_BLOCKS = 2
 
 FLOPS = 2 * 2 * TOKENS * F_OUT * F_IN
 
@@ -141,36 +142,36 @@ def tile_orthogonallyattenuatedlinear_t_v_kernel(
         def flip_ga(j):
             state(j)["ga_flipped"] = flip(state(j)["ga"][:], "ga_flipped")
 
-        def scaled_copy(source, factors, label):
-            scaled = deep.tile([P, PACK, P], F32, name=label, tag=label)
-            for b in range(PACK):
+        def scaled_copy(source, factors, label, blocks):
+            scaled = deep.tile([P, blocks, P], F32, name=label, tag=label)
+            for b in range(blocks):
                 nc.scalar.activation(
                     out=scaled[:, b, :], in_=source[:, b, :], func=ACT.Copy, scale=factors[:, b : b + 1]
                 )
             return scaled
 
-        def pp_on_gpsimd(j):
-            return j % 2 == 1 and j > 1
-
-        def scale_s(j):
+        def scale_pw(j):
             t = state(j)
-            t["pw_s"] = scaled_copy(t["pw_flipped"], two_over_sigma2, "pw_s")
+            t["pw_s"] = scaled_copy(t["pw_flipped"], two_over_sigma2, "pw_s", PACK)
 
-        def scale_k(j):
+        def scale_pwc(j):
             t = state(j)
-            if pp_on_gpsimd(j):
-                t["other"] = scaled_copy(t["pwc_flipped"], one_over_wnorm, "other")
-            else:
-                t["other"] = scaled_copy(t["pw_flipped"], two_over_sigma2_wnorm, "other")
+            t["pwc_n"] = scaled_copy(t["pwc_flipped"], one_over_wnorm, "pwc_n", GPSIMD_BLOCKS)
 
-        def make_pp(j):
+        def make_pp_gpsimd(j):
             t = state(j)
-            pp = deep.tile([P, PACK, P], F32, tag="pp")
-            if pp_on_gpsimd(j):
-                nc.gpsimd.tensor_tensor(out=pp[:], in0=t["pw_s"][:], in1=t["other"][:], op=MULT)
-            else:
-                nc.vector.tensor_tensor(out=pp[:], in0=t["other"][:], in1=t["pwc_flipped"][:], op=MULT)
-            t["pp"] = pp
+            t["pp"] = deep.tile([P, PACK, P], F32, name="pp", tag="pp")
+            nc.gpsimd.tensor_tensor(
+                out=t["pp"][:, 0:GPSIMD_BLOCKS, :], in0=t["pw_s"][:, 0:GPSIMD_BLOCKS, :], in1=t["pwc_n"][:], op=MULT
+            )
+
+        def make_pp_vector(j):
+            t = state(j)
+            for b in range(GPSIMD_BLOCKS, PACK):
+                nc.vector.scalar_tensor_tensor(
+                    out=t["pp"][:, b, :], in0=t["pwc_flipped"][:, b, :], scalar=one_over_wnorm[:, b : b + 1],
+                    in1=t["pw_s"][:, b, :], op0=MULT, op1=MULT,
+                )
 
         def make_h2(j):
             t = state(j)
@@ -261,10 +262,6 @@ def tile_orthogonallyattenuatedlinear_t_v_kernel(
         nc.vector.tensor_scalar_max(out=wnorm_floor[:], in0=wnorm[:], scalar1=1e-12)
         one_over_wnorm = consts.tile([P, PACK], F32)
         nc.vector.reciprocal(out=one_over_wnorm[:], in_=wnorm_floor[:])
-        two_over_sigma2_wnorm = consts.tile([P, PACK], F32)
-        nc.vector.tensor_tensor(
-            out=two_over_sigma2_wnorm[:], in0=two_over_sigma2[:], in1=one_over_wnorm[:], op=MULT
-        )
 
         c_grouped = consts.tile([P, F_IN, PACK], BF16, align_bytes=64)
         nc.vector.tensor_copy(out=c_grouped[:], in_=c_raw[:].rearrange("q b k -> q k b"))
@@ -283,16 +280,15 @@ def tile_orthogonallyattenuatedlinear_t_v_kernel(
             if in_range(c):
                 make_h2(c)
             if in_range(c + 2):
-                scale_s(c + 2)
+                scale_pw(c + 2)
                 flip_pwc(c + 2)
-            if in_range(c + 1) and not pp_on_gpsimd(c + 1):
-                make_pp(c + 1)
+            if in_range(c + 1):
+                make_pp_vector(c + 1)
             if in_range(c):
                 cast_h2(c)
             if in_range(c + 2):
-                scale_k(c + 2)
-                if pp_on_gpsimd(c + 2):
-                    make_pp(c + 2)
+                scale_pwc(c + 2)
+                make_pp_gpsimd(c + 2)
             if in_range(c):
                 back(c)
                 make_d(c)

@@ -21,6 +21,7 @@ PACK = 4
 TILES = TOKENS // P
 CHUNK = 2
 X_LAG = 2
+RUN = 4
 GPSIMD_BLOCKS = 2
 
 FLOPS = 2 * 2 * TOKENS * F_OUT * F_IN
@@ -111,7 +112,9 @@ def tile_orthogonallyattenuatedlinear_t_v_kernel(
         nc.scalar.sqrt(out=wnorm[:], in_=sum_squares[:])
 
         w_grouped = consts.tile([P, F_IN, PACK], BF16, align_bytes=64)
-        nc.vector.tensor_copy(out=w_grouped[:], in_=w_raw[:].rearrange("q b k -> q k b"))
+        nc.vector.tensor_copy(
+            out=w_grouped[:].rearrange("q (c i) b -> q c b i", i=RUN), in_=w_raw[:].rearrange("q b (c i) -> q c b i", i=RUN)
+        )
         w_codes, w_scales = quantise_matrix(w_grouped, "w")
 
         live = {}
@@ -182,7 +185,10 @@ def tile_orthogonallyattenuatedlinear_t_v_kernel(
 
         def cast_h2(j):
             t = state(j)
-            nc.scalar.copy(out=t["d_h2"][:, 1, :, :], in_=t["h2"][:].rearrange("q b r -> q r b"))
+            nc.scalar.copy(
+                out=t["d_h2"][:, 1, :, :].rearrange("q (c i) b -> q c b i", i=RUN),
+                in_=t["h2"][:].rearrange("q b (c i) -> q c b i", i=RUN),
+            )
 
         def back(j):
             t = state(j)
@@ -264,7 +270,9 @@ def tile_orthogonallyattenuatedlinear_t_v_kernel(
         nc.vector.reciprocal(out=one_over_wnorm[:], in_=wnorm_floor[:])
 
         c_grouped = consts.tile([P, F_IN, PACK], BF16, align_bytes=64)
-        nc.vector.tensor_copy(out=c_grouped[:], in_=c_raw[:].rearrange("q b k -> q k b"))
+        nc.vector.tensor_copy(
+            out=c_grouped[:].rearrange("q (c i) b -> q c b i", i=RUN), in_=c_raw[:].rearrange("q b (c i) -> q c b i", i=RUN)
+        )
 
         for c in range(-3, TILES + 2):
             if in_range(c - 1):

@@ -46,13 +46,13 @@ def tile_orthogonallyattenuatedlinear_t_v_kernel(
         sums = stack.enter_context(tc.psum_pool(name="sums", bufs=1))
         stack.enter_context(tc.manual_schedule())
 
-        sigma_rows_bf = consts.tile([P, P], BF16)
-        nc.vector.memset(sigma_rows_bf[:], 0.0)
-        nc.sync.dma_start(out=sigma_rows_bf[0:PACK, :], in_=sigma.rearrange("(b q) -> b q", q=P))
-
         w_raw = consts.tile([P, PACK, F_IN], BF16)
         c_raw = consts.tile([P, PACK, F_IN], BF16)
         nc.sync.dma_start(out=w_raw[:], in_=weights.rearrange("(b q) k -> q b k", q=P))
+
+        sigma_rows_bf = consts.tile([P, P], BF16)
+        nc.vector.memset(sigma_rows_bf[:], 0.0)
+        nc.sync.dma_start(out=sigma_rows_bf[0:PACK, :], in_=sigma.rearrange("(b q) -> b q", q=P))
 
         g_in, om_in, pw_in, pwc_in, x_in = {}, {}, {}, {}, {}
 

@@ -20,7 +20,8 @@ F_IN = 512
 PACK = 4
 TILES = TOKENS // P
 CHUNK = 2
-X_LAG = 2
+X_TILES = 2
+X_LAG = 3
 RUN = 4
 GPSIMD_BLOCKS = 2
 
@@ -32,8 +33,8 @@ def tile_orthogonallyattenuatedlinear_t_v_kernel(
 ):
     nc = tc.nc
 
-    def by_token_tile(ap):
-        return ap.rearrange("(q j) f -> q j f", j=TILES)
+    def by_partition(ap):
+        return ap.rearrange("(q j) f -> q (j f)", j=TILES)
 
     with ExitStack() as stack:
         consts = stack.enter_context(tc.tile_pool(name="consts", bufs=1))
@@ -56,21 +57,22 @@ def tile_orthogonallyattenuatedlinear_t_v_kernel(
 
         g_in, om_in, pw_in, pwc_in, x_in = {}, {}, {}, {}, {}
 
-        def load_tile(held, source, dtype, label, j):
-            loaded = inputs.tile([P, F_OUT], dtype, name="%s%d" % (label, j))
-            nc.sync.dma_start(out=loaded[:], in_=by_token_tile(source)[:, j, :])
-            held[j] = loaded[:]
+        def load(held, source, dtype, label, j, count):
+            loaded = inputs.tile([P, count * F_OUT], dtype, name="%s%d" % (label, j))
+            nc.sync.dma_start(out=loaded[:], in_=by_partition(source)[:, j * F_OUT : (j + count) * F_OUT])
+            for i in range(count):
+                held[j + i] = loaded[:, i * F_OUT : (i + 1) * F_OUT]
 
         for j in range(TILES + X_LAG):
             if j < TILES:
-                load_tile(pw_in, pw, F32, "pw", j)
-                load_tile(g_in, grad_out, BF16, "g", j)
-                load_tile(om_in, om, F32, "om", j)
-                load_tile(pwc_in, pwc, F32, "pwc", j)
+                load(pw_in, pw, F32, "pw", j, 1)
+                load(g_in, grad_out, BF16, "g", j, 1)
+                load(om_in, om, F32, "om", j, 1)
+                load(pwc_in, pwc, F32, "pwc", j, 1)
             if j == 0:
                 nc.sync.dma_start(out=c_raw[:], in_=center.rearrange("(b q) k -> q b k", q=P))
-            if j >= X_LAG:
-                load_tile(x_in, x, BF16, "x", j - X_LAG)
+            if j >= X_LAG and (j - X_LAG) % X_TILES == 0:
+                load(x_in, x, BF16, "x", j - X_LAG, X_TILES)
 
         identity = consts.tile([P, P], F32)
         make_identity(nc, identity[:])
@@ -246,17 +248,19 @@ def tile_orthogonallyattenuatedlinear_t_v_kernel(
             c, i = divmod(j, CHUNK)
             t = live.pop(j)
             if i == 0:
-                result_of_chunk[c] = results.tile([P, CHUNK, F_IN], F32, name="result")
+                result_of_chunk[c] = results.tile([P, CHUNK * F_IN], F32, name="result")
             result = result_of_chunk[c]
             nc.vector.scalar_tensor_tensor(
-                out=result[:, i, :], in0=x_in[j], scalar=t["minus_rowsum"][:],
+                out=result[:, i * F_IN : (i + 1) * F_IN], in0=x_in[j], scalar=t["minus_rowsum"][:],
                 in1=t["acc"][:], op0=MULT, op1=ADD,
             )
             if c == TILES // CHUNK - 1:
-                nc.sync.dma_start(out=by_token_tile(out)[:, j, :], in_=result[:, i, :])
+                nc.sync.dma_start(
+                    out=by_partition(out)[:, j * F_IN : (j + 1) * F_IN], in_=result[:, i * F_IN : (i + 1) * F_IN]
+                )
             elif i == CHUNK - 1:
                 nc.sync.dma_start(
-                    out=by_token_tile(out)[:, c * CHUNK : (c + 1) * CHUNK, :], in_=result[:]
+                    out=by_partition(out)[:, c * CHUNK * F_IN : (c + 1) * CHUNK * F_IN], in_=result[:]
                 )
 
         def in_range(j):
@@ -281,7 +285,7 @@ def tile_orthogonallyattenuatedlinear_t_v_kernel(
                 flip_pw(c + 2)
             if in_range(c + 1):
                 flip_ga(c + 1)
-            if in_range(c + 3) and c + 3 > 0:
+            if 0 < c + 3 and c < 0:
                 make_ga(c + 3)
             if in_range(c - 1):
                 multiply(c - 1)
@@ -297,6 +301,8 @@ def tile_orthogonallyattenuatedlinear_t_v_kernel(
             if in_range(c + 2):
                 scale_pwc(c + 2)
                 make_pp_gpsimd(c + 2)
+            if in_range(c + 3) and c >= 0:
+                make_ga(c + 3)
             if in_range(c):
                 back(c)
                 make_d(c)

@@ -68,9 +68,9 @@ def tile_orthogonallyattenuatedlinear_t_v_kernel(
                 load(pw_in, pw, F32, "pw", j, 1)
                 load(g_in, grad_out, BF16, "g", j, 1)
                 load(om_in, om, F32, "om", j, 1)
+                if j == 0:
+                    nc.sync.dma_start(out=c_raw[:], in_=center.rearrange("(b q) k -> q b k", q=P))
                 load(pwc_in, pwc, F32, "pwc", j, 1)
-            if j == 0:
-                nc.sync.dma_start(out=c_raw[:], in_=center.rearrange("(b q) k -> q b k", q=P))
             if j >= X_LAG and (j - X_LAG) % X_TILES == 0:
                 load(x_in, x, BF16, "x", j - X_LAG, X_TILES)
 
@@ -132,6 +132,9 @@ def tile_orthogonallyattenuatedlinear_t_v_kernel(
                 nc.tensor.transpose(bank[:, b, :], source[:, b * P : (b + 1) * P], identity[:])
             return bank
 
+        def gpsimd_blocks(j):
+            return 0 if j == 0 else GPSIMD_BLOCKS
+
         def make_ga(j):
             ga = work.tile([P, F_OUT], F32, tag="ga")
             engine = nc.vector if j == 0 else nc.gpsimd
@@ -161,18 +164,20 @@ def tile_orthogonallyattenuatedlinear_t_v_kernel(
 
         def scale_pwc(j):
             t = state(j)
-            t["pwc_n"] = scaled_copy(t["pwc_flipped"], one_over_wnorm, "pwc_n", GPSIMD_BLOCKS)
+            if gpsimd_blocks(j) > 0:
+                t["pwc_n"] = scaled_copy(t["pwc_flipped"], one_over_wnorm, "pwc_n", GPSIMD_BLOCKS)
 
         def make_pp_gpsimd(j):
             t = state(j)
             t["pp"] = deep.tile([P, PACK, P], F32, name="pp", tag="pp")
-            nc.gpsimd.tensor_tensor(
-                out=t["pp"][:, 0:GPSIMD_BLOCKS, :], in0=t["pw_s"][:, 0:GPSIMD_BLOCKS, :], in1=t["pwc_n"][:], op=MULT
-            )
+            if gpsimd_blocks(j) > 0:
+                nc.gpsimd.tensor_tensor(
+                    out=t["pp"][:, 0:GPSIMD_BLOCKS, :], in0=t["pw_s"][:, 0:GPSIMD_BLOCKS, :], in1=t["pwc_n"][:], op=MULT
+                )
 
         def make_pp_vector(j):
             t = state(j)
-            for b in range(GPSIMD_BLOCKS, PACK):
+            for b in range(gpsimd_blocks(j), PACK):
                 nc.vector.scalar_tensor_tensor(
                     out=t["pp"][:, b, :], in0=t["pwc_flipped"][:, b, :], scalar=one_over_wnorm[:, b : b + 1],
                     in1=t["pw_s"][:, b, :], op0=MULT, op1=MULT,
@@ -250,15 +255,19 @@ def tile_orthogonallyattenuatedlinear_t_v_kernel(
             if i == 0:
                 result_of_chunk[c] = results.tile([P, CHUNK * F_IN], F32, name="result")
             result = result_of_chunk[c]
-            nc.vector.scalar_tensor_tensor(
-                out=result[:, i * F_IN : (i + 1) * F_IN], in0=x_in[j], scalar=t["minus_rowsum"][:],
-                in1=t["acc"][:], op0=MULT, op1=ADD,
-            )
-            if c == TILES // CHUNK - 1:
-                nc.sync.dma_start(
-                    out=by_partition(out)[:, j * F_IN : (j + 1) * F_IN], in_=result[:, i * F_IN : (i + 1) * F_IN]
+            parts = 2 if j == TILES - 1 else 1
+            for part in range(parts):
+                cols = slice(part * F_IN // parts, (part + 1) * F_IN // parts)
+                at = slice(i * F_IN + cols.start, i * F_IN + cols.stop)
+                nc.vector.scalar_tensor_tensor(
+                    out=result[:, at], in0=x_in[j][:, cols], scalar=t["minus_rowsum"][:],
+                    in1=t["acc"][:][:, cols], op0=MULT, op1=ADD,
                 )
-            elif i == CHUNK - 1:
+                if c == TILES // CHUNK - 1:
+                    nc.sync.dma_start(
+                        out=by_partition(out)[:, j * F_IN + cols.start : j * F_IN + cols.stop], in_=result[:, at]
+                    )
+            if c < TILES // CHUNK - 1 and i == CHUNK - 1:
                 nc.sync.dma_start(
                     out=by_partition(out)[:, c * CHUNK * F_IN : (c + 1) * CHUNK * F_IN], in_=result[:]
                 )
@@ -277,6 +286,8 @@ def tile_orthogonallyattenuatedlinear_t_v_kernel(
         nc.vector.tensor_copy(
             out=c_grouped[:].rearrange("q (c i) b -> q c b i", i=RUN), in_=c_raw[:].rearrange("q b (c i) -> q c b i", i=RUN)
         )
+
+        center_mx.extend(quantise_matrix(c_grouped, "c"))
 
         for c in range(-3, TILES + 2):
             if in_range(c - 1):
@@ -307,7 +318,5 @@ def tile_orthogonallyattenuatedlinear_t_v_kernel(
                 back(c)
                 make_d(c)
                 rowsum(c)
-            if c == 0:
-                center_mx.extend(quantise_matrix(c_grouped, "c"))
             if in_range(c - 1):
                 finish(c - 1)

from contextlib import ExitStack

import concourse.mybir as mybir
from concourse.masks import make_identity

F32 = mybir.dt.float32
BF16 = mybir.dt.bfloat16
U32 = mybir.dt.uint32
U8 = mybir.dt.uint8
E4M3_X4 = mybir.dt.float8_e4m3fn_x4
E5M2_X4 = mybir.dt.float8_e5m2_x4
MULT = mybir.AluOpType.mult
ADD = mybir.AluOpType.add
ACT = mybir.ActivationFunctionType

P = 128
TOKENS = 2048
F_OUT = 512
F_IN = 512
PACK = 4
TILES = TOKENS // P
CHUNK = 2
X_TILES = 2
X_LAG = 3
RUN = 4
GPSIMD_BLOCKS = 2

FLOPS = 2 * 2 * TOKENS * F_OUT * F_IN


def tile_orthogonallyattenuatedlinear_t_v_kernel(
    tc, x, weights, bias, center, sigma, pw, pwc, om, grad_out, out
):
    nc = tc.nc

    def by_partition(ap):
        return ap.rearrange("(q j) f -> q (j f)", j=TILES)

    with ExitStack() as stack:
        consts = stack.enter_context(tc.tile_pool(name="consts", bufs=1))
        inputs = stack.enter_context(tc.tile_pool(name="inputs", bufs=1))
        work = stack.enter_context(tc.tile_pool(name="work", bufs=2))
        deep = stack.enter_context(tc.tile_pool(name="deep", bufs=3))
        small = stack.enter_context(tc.tile_pool(name="small", bufs=4))
        results = stack.enter_context(tc.tile_pool(name="results", bufs=TILES // CHUNK))
        flipped = stack.enter_context(tc.psum_pool(name="flipped", bufs=2))
        sums = stack.enter_context(tc.psum_pool(name="sums", bufs=1))
        stack.enter_context(tc.manual_schedule())

        w_raw = consts.tile([P, PACK, F_IN], BF16)
        c_raw = consts.tile([P, PACK, F_IN], BF16)
        nc.sync.dma_start(out=w_raw[:], in_=weights.rearrange("(b q) k -> q b k", q=P))

        sigma_rows_bf = consts.tile([P, P], BF16)
        nc.vector.memset(sigma_rows_bf[:], 0.0)
        nc.sync.dma_start(out=sigma_rows_bf[0:PACK, :], in_=sigma.rearrange("(b q) -> b q", q=P))

        g_in, om_in, pw_in, pwc_in, x_in = {}, {}, {}, {}, {}

        def load(held, source, dtype, label, j, count):
            loaded = inputs.tile([P, count * F_OUT], dtype, name="%s%d" % (label, j))
            nc.sync.dma_start(out=loaded[:], in_=by_partition(source)[:, j * F_OUT : (j + count) * F_OUT])
            for i in range(count):
                held[j + i] = loaded[:, i * F_OUT : (i + 1) * F_OUT]

        for j in range(TILES + X_LAG):
            if j < TILES:
                load(pw_in, pw, F32, "pw", j, 1)
                load(g_in, grad_out, BF16, "g", j, 1)
                load(om_in, om, F32, "om", j, 1)
                if j == 0:
                    nc.sync.dma_start(out=c_raw[:], in_=center.rearrange("(b q) k -> q b k", q=P))
                load(pwc_in, pwc, F32, "pwc", j, 1)
            if j >= X_LAG and (j - X_LAG) % X_TILES == 0:
                load(x_in, x, BF16, "x", j - X_LAG, X_TILES)

        identity = consts.tile([P, P], F32)
        make_identity(nc, identity[:])

        warm = consts.tile([P, 1], F32)
        nc.vector.memset(warm[:], 1.0)
        nc.scalar.sqrt(out=warm[:], in_=warm[:])

        sigma_rows = consts.tile([P, P], F32)
        nc.vector.tensor_copy(out=sigma_rows[:], in_=sigma_rows_bf[:])
        sigma_flipped = flipped.tile([P, PACK, P], F32, tag="pw_flipped")
        nc.tensor.transpose(sigma_flipped[:, 0, :], sigma_rows[:], identity[:])
        sigma_cols = consts.tile([P, PACK], F32)
        nc.vector.tensor_copy(out=sigma_cols[:], in_=sigma_flipped[:, 0, 0:PACK])
        half_sigma2 = consts.tile([P, PACK], F32)
        nc.vector.scalar_tensor_tensor(
            out=half_sigma2[:], in0=sigma_cols[:], scalar=0.5, in1=sigma_cols[:], op0=MULT, op1=MULT
        )
        two_over_sigma2 = consts.tile([P, PACK], F32)
        nc.vector.reciprocal(out=two_over_sigma2[:], in_=half_sigma2[:])

        def quantise_matrix(grouped, label):
            codes = consts.tile([P, F_IN], U32, align_bytes=64, name=label + "_codes")
            scales = consts.tile([P, F_IN], U8, align_bytes=64, name=label + "_scales")
            nc.vector.quantize_mx(
                out=codes[:].bitcast(E4M3_X4), scales=scales[:],
                in_=grouped[:].rearrange("q k b -> q (k b)"),
            )
            return codes, scales

        squares = consts.tile([P, PACK, F_IN], BF16)
        sum_squares = consts.tile([P, PACK], F32)
        for b in range(PACK):
            nc.scalar.activation(
                out=squares[:, b, :], in_=w_raw[:, b, :], func=ACT.Square,
                accum_out=sum_squares[:, b : b + 1],
            )
        wnorm = consts.tile([P, PACK], F32)
        nc.scalar.sqrt(out=wnorm[:], in_=sum_squares[:])

        w_grouped = consts.tile([P, F_IN, PACK], BF16, align_bytes=64)
        nc.vector.tensor_copy(
            out=w_grouped[:].rearrange("q (c i) b -> q c b i", i=RUN), in_=w_raw[:].rearrange("q b (c i) -> q c b i", i=RUN)
        )
        w_codes, w_scales = quantise_matrix(w_grouped, "w")

        live = {}
        center_mx = []
        result_of_chunk = {}

        def state(j):
            return live.setdefault(j, {})

        def flip(source, label):
            bank = flipped.tile([P, PACK, P], F32, name=label, tag=label)
            for b in range(PACK):
                nc.tensor.transpose(bank[:, b, :], source[:, b * P : (b + 1) * P], identity[:])
            return bank

        def gpsimd_blocks(j):
            return 0 if j == 0 else GPSIMD_BLOCKS

        def make_ga(j):
            ga = work.tile([P, F_OUT], F32, tag="ga")
            engine = nc.vector if j == 0 else nc.gpsimd
            engine.tensor_tensor(out=ga[:], in0=g_in[j], in1=om_in[j], op=MULT)
            state(j)["ga"] = ga

        def flip_pw(j):
            state(j)["pw_flipped"] = flip(pw_in[j], "pw_flipped")

        def flip_pwc(j):
            state(j)["pwc_flipped"] = flip(pwc_in[j], "pwc_flipped")

        def flip_ga(j):
            state(j)["ga_flipped"] = flip(state(j)["ga"][:], "ga_flipped")

        def scaled_copy(source, factors, label, blocks):
            scaled = deep.tile([P, blocks, P], F32, name=label, tag=label)
            for b in range(blocks):
                nc.scalar.activation(
                    out=scaled[:, b, :], in_=source[:, b, :], func=ACT.Copy, scale=factors[:, b : b + 1]
                )
            return scaled

        def scale_pw(j):
            t = state(j)
            t["pw_s"] = scaled_copy(t["pw_flipped"], two_over_sigma2, "pw_s", PACK)

        def scale_pwc(j):
            t = state(j)
            if gpsimd_blocks(j) > 0:
                t["pwc_n"] = scaled_copy(t["pwc_flipped"], one_over_wnorm, "pwc_n", GPSIMD_BLOCKS)

        def make_pp_gpsimd(j):
            t = state(j)
            t["pp"] = deep.tile([P, PACK, P], F32, name="pp", tag="pp")
            if gpsimd_blocks(j) > 0:
                nc.gpsimd.tensor_tensor(
                    out=t["pp"][:, 0:GPSIMD_BLOCKS, :], in0=t["pw_s"][:, 0:GPSIMD_BLOCKS, :], in1=t["pwc_n"][:], op=MULT
                )

        def make_pp_vector(j):
            t = state(j)
            for b in range(gpsimd_blocks(j), PACK):
                nc.vector.scalar_tensor_tensor(
                    out=t["pp"][:, b, :], in0=t["pwc_flipped"][:, b, :], scalar=one_over_wnorm[:, b : b + 1],
                    in1=t["pw_s"][:, b, :], op0=MULT, op1=MULT,
                )

        def make_h2(j):
            t = state(j)
            h2 = work.tile([P, PACK, P], F32, tag="h2")
            nc.vector.tensor_tensor(out=h2[:], in0=t["pw_s"][:], in1=t["ga_flipped"][:], op=MULT)
            t["h2"] = h2
            t["d_h2"] = deep.tile([P, 2, P, PACK], BF16, align_bytes=64, name="d_h2", tag="d_h2")

        def cast_h2(j):
            t = state(j)
            nc.scalar.copy(
                out=t["d_h2"][:, 1, :, :].rearrange("q (c i) b -> q c b i", i=RUN),
                in_=t["h2"][:].rearrange("q b (c i) -> q c b i", i=RUN),
            )

        def back(j):
            t = state(j)
            h2_by_token = sums.tile([P, P], F32, tag="h2_by_token")
            for b in range(PACK):
                nc.tensor.matmul(
                    h2_by_token[:], lhsT=t["h2"][:, b, :], rhs=identity[:], is_transpose=True,
                    start=(b == 0), stop=(b == PACK - 1),
                )
            t["h2_by_token"] = h2_by_token

        def make_d(j):
            t = state(j)
            nc.vector.scalar_tensor_tensor(
                out=t["d_h2"][:, 0, :, :], in0=t["pp"][:].rearrange("q b r -> q r b"), scalar=1.0,
                in1=t["ga_flipped"][:].rearrange("q b r -> q r b"), op0=ADD, op1=MULT,
            )

        def rowsum(j):
            t = state(j)
            minus_rowsum = small.tile([P, 1], F32, tag="minus_rowsum")
            unread = work.tile([P, P], BF16, tag="unread")
            nc.scalar.activation(
                out=unread[:], in_=t["h2_by_token"][:], func=ACT.Copy, scale=-1.0,
                accum_out=minus_rowsum[:],
            )
            t["minus_rowsum"] = minus_rowsum

        def quantise(j):
            t = state(j)
            codes = work.tile([P, 2 * P], U32, align_bytes=64, tag="codes")
            scales = work.tile([P, 2 * P], U8, align_bytes=64, tag="scales")
            nc.vector.quantize_mx(
                out=codes[:].bitcast(E5M2_X4), scales=scales[:],
                in_=t["d_h2"][:].rearrange("q s r b -> q (s r b)"),
            )
            t["codes"] = codes
            t["scales"] = scales

        def multiply(j):
            t = state(j)
            codes, scales = t["codes"], t["scales"]
            acc = sums.tile([P, F_IN], F32, tag="acc")
            nc.tensor.matmul_mx(
                out=acc[:], lhsT=codes[:, 0:P].bitcast(E5M2_X4), lhsT_scale=scales[:, 0:P],
                rhs=w_codes[:].bitcast(E4M3_X4), rhs_scale=w_scales[:], start=True, stop=False,
            )
            nc.tensor.matmul_mx(
                out=acc[:], lhsT=codes[:, P : 2 * P].bitcast(E5M2_X4), lhsT_scale=scales[:, P : 2 * P],
                rhs=center_mx[0][:].bitcast(E4M3_X4), rhs_scale=center_mx[1][:], start=False, stop=True,
            )
            t["acc"] = acc

        def finish(j):
            c, i = divmod(j, CHUNK)
            t = live.pop(j)
            if i == 0:
                result_of_chunk[c] = results.tile([P, CHUNK * F_IN], F32, name="result")
            result = result_of_chunk[c]
            parts = 2 if j == TILES - 1 else 1
            for part in range(parts):
                cols = slice(part * F_IN // parts, (part + 1) * F_IN // parts)
                at = slice(i * F_IN + cols.start, i * F_IN + cols.stop)
                nc.vector.scalar_tensor_tensor(
                    out=result[:, at], in0=x_in[j][:, cols], scalar=t["minus_rowsum"][:],
                    in1=t["acc"][:][:, cols], op0=MULT, op1=ADD,
                )
                if c == TILES // CHUNK - 1:
                    nc.sync.dma_start(
                        out=by_partition(out)[:, j * F_IN + cols.start : j * F_IN + cols.stop], in_=result[:, at]
                    )
            if c < TILES // CHUNK - 1 and i == CHUNK - 1:
                nc.sync.dma_start(
                    out=by_partition(out)[:, c * CHUNK * F_IN : (c + 1) * CHUNK * F_IN], in_=result[:]
                )

        def in_range(j):
            return 0 <= j < TILES

        make_ga(0)

        wnorm_floor = consts.tile([P, PACK], F32)
        nc.vector.tensor_scalar_max(out=wnorm_floor[:], in0=wnorm[:], scalar1=1e-12)
        one_over_wnorm = consts.tile([P, PACK], F32)
        nc.vector.reciprocal(out=one_over_wnorm[:], in_=wnorm_floor[:])

        c_grouped = consts.tile([P, F_IN, PACK], BF16, align_bytes=64)
        nc.vector.tensor_copy(
            out=c_grouped[:].rearrange("q (c i) b -> q c b i", i=RUN), in_=c_raw[:].rearrange("q b (c i) -> q c b i", i=RUN)
        )

        center_mx.extend(quantise_matrix(c_grouped, "c"))

        for c in range(-3, TILES + 2):
            if in_range(c - 1):
                quantise(c - 1)
            if in_range(c + 2):
                flip_pw(c + 2)
            if in_range(c + 1):
                flip_ga(c + 1)
            if 0 < c + 3 and c < 0:
                make_ga(c + 3)
            if in_range(c - 1):
                multiply(c - 1)
            if in_range(c):
                make_h2(c)
            if in_range(c + 2):
                scale_pw(c + 2)
                flip_pwc(c + 2)
            if in_range(c + 1):
                make_pp_vector(c + 1)
            if in_range(c):
                cast_h2(c)
            if in_range(c + 2):
                scale_pwc(c + 2)
                make_pp_gpsimd(c + 2)
            if in_range(c + 3) and c >= 0:
                make_ga(c + 3)
            if in_range(c):
                back(c)
                make_d(c)
                rowsum(c)
            if in_range(c - 1):
                finish(c - 1)
